import numpy as np
import ml_dtypes


def mxq(x, axis, fmt="e4m3"):
    dtype, down = {"e4m3": (ml_dtypes.float8_e4m3fn, 7), "e5m2": (ml_dtypes.float8_e5m2, 14)}[fmt]
    v = np.moveaxis(np.asarray(x, np.float32).astype(ml_dtypes.bfloat16).astype(np.float64), axis, -1)
    blocks = v.reshape(v.shape[:-1] + (-1, 32))
    amax = np.abs(blocks).max(-1, keepdims=True)
    byte = np.maximum(np.where(amax > 0, np.frexp(amax)[1] - 1 + 127, 0) - down, 1)
    scale = np.exp2(byte - 127.0)
    codes = (blocks / scale).astype(np.float32).astype(dtype).astype(np.float64)
    return np.moveaxis((codes * scale).reshape(v.shape), -1, axis)


WIDE = False


def mx_kscale(k):
    if not WIDE:
        return np.ones(k)
    levels = np.array([10, -10, 5, -5, 0])
    a = np.random.permutation(np.resize(levels, k // 512 * 4)).reshape(k // 512, 4)
    idx = np.arange(k)
    return np.exp2(a[idx // 512, idx % 128 // 32])


BF16 = ml_dtypes.bfloat16


def bf(x):
    return np.asarray(x, np.float32).astype(BF16)


def f64(x):
    return np.asarray(x).astype(np.float64)


N, E, D = 4096, 4096, 128


def setup_inputs():
    s = mx_kscale(N)
    s = s / np.exp2(np.round(np.log2(s.mean())))
    return {"X": bf(np.random.standard_normal((N, D)) * 0.5 * np.sqrt(N) / s[:, None]),
            "H": bf(np.random.uniform(0.0, 1.0, (N, E)) * (16.0 / N) * s[:, None])}


def reference(X, H):
    Hf = f64(H)
    msg = mxq(Hf, 0, "e4m3").T @ mxq(f64(X), 0, "e4m3")
    with np.errstate(divide="ignore"):
        inv_deg = 1.0 / Hf.sum(axis=0)
    inv_deg = np.where(np.isinf(inv_deg), 0.0, inv_deg)
    return msg * inv_deg[:, None]

@@ -1,0 +1,246 @@
+from contextlib import ExitStack
+
+import concourse.mybir as mybir
+
+BF16 = mybir.dt.bfloat16
+F32 = mybir.dt.float32
+U32 = mybir.dt.uint32
+U8 = mybir.dt.uint8
+FP8X4 = mybir.dt.float8_e4m3fn_x4
+ALU = mybir.AluOpType
+ACT = mybir.ActivationFunctionType
+
+P = 128
+PACK = 4
+K_PASS = P * PACK
+N_VERT = 4096
+N_EDGE = 4096
+D = 128
+PASSES = N_VERT // K_PASS
+BANK_COLS = 512
+TILES_PER_BANK = BANK_COLS // P
+UNIT = 1024
+NDEG = 12
+
+FLOPS = 2 * N_VERT * N_EDGE * D
+
+BLOCKS = [(0, 2048), (2048, 2048)]
+HEAD_WIDTHS = [512, 512, 1024]
+TAIL_WIDTHS = [1024, 512, 512]
+RAW_BUFS = 6
+GRP_BUFS = 3
+CODE_BUFS = 4
+OUT_BUFS = 4
+V_SHARE = {1024: 528, 512: 264}
+V_SHARE_LAST = 344
+X_V_PASSES = 6
+
+
+def make_pieces():
+    pieces = []
+    for b, (b0, bw) in enumerate(BLOCKS):
+        for c in range(PASSES):
+            widths = [bw]
+            if b == 0 and c == 0:
+                widths = HEAD_WIDTHS
+            if b == len(BLOCKS) - 1 and c == PASSES - 1:
+                widths = TAIL_WIDTHS
+            off = b0
+            for w in widths:
+                pieces.append({"b": b, "c": c, "e0": off, "w": w, "last_in_pass": off + w == b0 + bw})
+                off += w
+    return pieces
+
+
+def make_units(pieces):
+    units = []
+    for k, pc in enumerate(pieces):
+        n_u = max(1, pc["w"] // UNIT)
+        uw = pc["w"] // n_u
+        for i in range(n_u):
+            units.append({"k": k, "off": i * uw, "w": uw, "first": i == 0, "last": i == n_u - 1})
+    return units
+
+
+def tile_v2emsgpass_kernel(tc, X, H, out):
+    nc = tc.nc
+    pieces = make_pieces()
+    units = make_units(pieces)
+    n_units = len(units)
+    h_view = H.rearrange("(c p j) e -> c p j e", p=P, j=PACK)
+
+    with ExitStack() as ctx:
+        ctx.enter_context(tc.manual_schedule())
+        const = ctx.enter_context(tc.tile_pool(name="const", bufs=1))
+        raw_pool = ctx.enter_context(tc.tile_pool(name="rawp", bufs=RAW_BUFS))
+        grp_pool = ctx.enter_context(tc.tile_pool(name="grpp", bufs=GRP_BUFS))
+        code_pool = ctx.enter_context(tc.tile_pool(name="codep", bufs=CODE_BUFS))
+        out_pool = ctx.enter_context(tc.tile_pool(name="outp", bufs=OUT_BUFS))
+        mx_psum = ctx.enter_context(tc.psum_pool(name="mxps", bufs=6))
+        deg_psum = ctx.enter_context(tc.psum_pool(name="degps", bufs=2))
+
+        ones = const.tile([P, NDEG], BF16, name="ones")
+        nc.vector.memset(ones[:], 1.0)
+        n_tiles = N_EDGE // P
+        d1 = const.tile([P, n_tiles], F32, name="d1")
+        dg = const.tile([P, n_tiles], F32, name="dg")
+        sf = const.tile([P, n_tiles], F32, name="sf")
+        rc = const.tile([P, n_tiles], F32, name="rc")
+        inv = const.tile([P, n_tiles], F32, name="inv")
+
+        raw_tiles = {}
+
+        def load(k):
+            pc = pieces[k]
+            raw = raw_pool.tile([P, PACK, pc["w"]], BF16, name="raw", tag="raw")
+            nc.sync.dma_start(out=raw[:], in_=h_view[pc["c"], :, :, pc["e0"] : pc["e0"] + pc["w"]])
+            raw_tiles[k] = raw
+
+        x_raw = const.tile([P, PASSES, PACK, D], BF16, name="x_raw")
+        nc.sync.dma_start(out=x_raw[:], in_=X.rearrange("(c p j) d -> p c j d", p=P, j=PACK))
+        for k in range(RAW_BUFS):
+            load(k)
+        x_grp = const.tile([P, PASSES, D, PACK], BF16, name="x_grp", align_bytes=64)
+        nc.vector.tensor_copy(
+            out=x_grp[:, :X_V_PASSES], in_=x_raw[:, :X_V_PASSES].rearrange("p c j d -> p c d j")
+        )
+        nc.scalar.copy(out=x_grp[:, X_V_PASSES:], in_=x_raw[:, X_V_PASSES:].rearrange("p c j d -> p c d j"))
+        x_codes = const.tile([P, PASSES, D], U32, name="x_codes", align_bytes=64)
+        x_scales = const.tile([P, PASSES, D], U8, name="x_scales", align_bytes=64)
+        nc.vector.quantize_mx(
+            out=x_codes[:].rearrange("p c d -> p (c d)").bitcast(FP8X4),
+            scales=x_scales[:].rearrange("p c d -> p (c d)"),
+            in_=x_grp[:].rearrange("p c d j -> p (c d j)"),
+        )
+
+        deg_tiles = {}
+        banks = {}
+        grp_tiles = {}
+
+        def degree_matmuls(k):
+            pc = pieces[k]
+            b, c = pc["b"], pc["c"]
+            b0, bw = BLOCKS[b]
+            phase = 1 if c == PASSES - 1 else 0
+            if (b, phase) not in deg_tiles:
+                deg_tiles[(b, phase)] = deg_psum.tile([P, bw // P, NDEG], F32, name="deg", tag="deg")
+            dt_ = deg_tiles[(b, phase)]
+            raw = raw_tiles[k]
+            n_t = pc["w"] // P
+            for t in range(n_t):
+                lt = (pc["e0"] - b0) // P + t
+                for j in range(PACK):
+                    first = t == 0 and j == 0
+                    final = t == n_t - 1 and j == PACK - 1
+                    if phase == 0:
+                        start = first and c == 0 and pc["e0"] == b0
+                        stop = final and c == PASSES - 2 and pc["last_in_pass"]
+                    else:
+                        start = first
+                        stop = final
+                    nc.tensor.matmul(
+                        out=dt_[:, lt, :],
+                        lhsT=raw[:, j, t * P : (t + 1) * P],
+                        rhs=ones[:],
+                        start=start,
+                        stop=stop,
+                    )
+
+        def regroup(s):
+            u = units[s]
+            k = u["k"]
+            if u["first"]:
+                degree_matmuls(k)
+            raw = raw_tiles[k]
+            w = u["w"]
+            cv = V_SHARE_LAST if s == n_units - 1 else V_SHARE[w]
+            g = grp_pool.tile([P, w, PACK], BF16, name="grp", tag="grp", align_bytes=64)
+            o = u["off"]
+            nc.vector.tensor_copy(
+                out=g[:, 0:cv, :].rearrange("p (c i) t -> p c t i", i=4),
+                in_=raw[:, :, o : o + cv].rearrange("p t (c i) -> p c t i", i=4),
+            )
+            nc.scalar.copy(
+                out=g[:, cv:w, :].rearrange("p (c i) t -> p c t i", i=4),
+                in_=raw[:, :, o + cv : o + w].rearrange("p t (c i) -> p c t i", i=4),
+            )
+            grp_tiles[s] = g
+            if u["last"] and k + RAW_BUFS < len(pieces):
+                load(k + RAW_BUFS)
+
+        def quantise_and_multiply(s):
+            u = units[s]
+            pc = pieces[u["k"]]
+            b, c = pc["b"], pc["c"]
+            b0, bw = BLOCKS[b]
+            w = u["w"]
+            g = grp_tiles[s]
+            codes = code_pool.tile([P, w], U32, name="codes", tag="codes", align_bytes=64)
+            scales = code_pool.tile([P, w], U8, name="scales", tag="scales", align_bytes=64)
+            nc.vector.quantize_mx(
+                out=codes[:].bitcast(FP8X4), scales=scales[:], in_=g[:].rearrange("p w j -> p (w j)")
+            )
+            e0 = pc["e0"] + u["off"]
+            closed = []
+            for t in range(w // P):
+                te = e0 // P + t
+                bank_id = te // TILES_PER_BANK
+                slot = te % TILES_PER_BANK
+                if c == 0 and slot == 0:
+                    banks[bank_id] = mx_psum.tile([P, BANK_COLS], F32, name="acc", tag="acc")
+                nc.tensor.matmul_mx(
+                    out=banks[bank_id][:, slot * P : (slot + 1) * P],
+                    lhsT=codes[:, t * P : (t + 1) * P].bitcast(FP8X4),
+                    lhsT_scale=scales[:, t * P : (t + 1) * P],
+                    rhs=x_codes[:, c, :].bitcast(FP8X4),
+                    rhs_scale=x_scales[:, c, :],
+                    start=(c == 0 and slot == 0),
+                    stop=(c == PASSES - 1 and slot == TILES_PER_BANK - 1),
+                )
+                if c == PASSES - 1 and slot == TILES_PER_BANK - 1:
+                    closed.append(bank_id)
+            if c == PASSES - 2 and pc["last_in_pass"] and u["last"]:
+                ta, tb = b0 // P, (b0 + bw) // P
+                nc.vector.tensor_copy(out=d1[:, ta:tb], in_=deg_tiles[(b, 0)][:, :, 0])
+            if c == PASSES - 1 and u["first"]:
+                ta, tb = pc["e0"] // P, (pc["e0"] + pc["w"]) // P
+                la, lb = ta - b0 // P, tb - b0 // P
+                nc.vector.tensor_tensor(
+                    out=dg[:, ta:tb], in0=deg_tiles[(b, 1)][:, la:lb, 0], in1=d1[:, ta:tb], op=ALU.add
+                )
+                nc.vector.scalar_tensor_tensor(
+                    out=sf[:, ta:tb], in0=dg[:, ta:tb], scalar=0.0, in1=dg[:, ta:tb],
+                    op0=ALU.is_equal, op1=ALU.add,
+                )
+                nc.vector.reciprocal(out=rc[:, ta:tb], in_=sf[:, ta:tb])
+                nc.vector.scalar_tensor_tensor(
+                    out=inv[:, ta:tb], in0=dg[:, ta:tb], scalar=0.0, in1=rc[:, ta:tb],
+                    op0=ALU.not_equal, op1=ALU.mult,
+                )
+            return closed
+
+        def evacuate(bank_id):
+            acc = banks[bank_id]
+            res = out_pool.tile([P, TILES_PER_BANK, D], F32, name="res", tag="res")
+            for slot in range(TILES_PER_BANK):
+                te = bank_id * TILES_PER_BANK + slot
+                nc.scalar.activation(
+                    out=res[:, slot, :],
+                    in_=acc[:, slot * P : (slot + 1) * P],
+                    func=ACT.Copy,
+                    scale=inv[:, te : te + 1],
+                )
+            e0 = bank_id * BANK_COLS
+            nc.scalar.dma_start(
+                out=out[e0 : e0 + BANK_COLS, :].rearrange("(s p) d -> p s d", p=P), in_=res[:]
+            )
+
+        closed_prev = []
+        for s in range(n_units + 2):
+            if s < n_units:
+                regroup(s)
+            for bank_id in closed_prev:
+                evacuate(bank_id)
+            closed_prev = []
+            if 1 <= s <= n_units:
+                closed_prev = quantise_and_multiply(s - 1)

@@ -17,8 +17,6 @@ N_VERT = 4096
 N_EDGE = 4096
 D = 128
 PASSES = N_VERT // K_PASS
-BANK_COLS = 512
-TILES_PER_BANK = BANK_COLS // P
 UNIT = 1024
 NDEG = 12
 
@@ -26,29 +24,64 @@ FLOPS = 2 * N_VERT * N_EDGE * D
 
 BLOCKS = [(0, 2048), (2048, 2048)]
 HEAD_WIDTHS = [512, 512, 1024]
-TAIL_WIDTHS = [1024, 512, 512]
+TAIL_WIDTHS = [1024, 512, 256, 256]
+GROUPS = [[512, 512, 512, 512], [512, 512, 512, 256, 256]]
 RAW_BUFS = 6
-GRP_BUFS = 3
-CODE_BUFS = 4
-OUT_BUFS = 4
-V_SHARE = {1024: 528, 512: 264}
-V_SHARE_LAST = 344
+GRP_BUFS = 4
+CODE_BUFS = 6
+OUT_BUFS = 8
+MX_BANKS = 6
+V_FRAC = 0.49
+V_FRAC_EVAC = 0.7
+V_FRAC_TAIL = [0.4, 0.4, 0.4, 0.45]
 X_V_PASSES = 6
+X_AFTER = 1
+DEG_AHEAD = 1
+DEFER_STORES = True
+TAIL_PASSES = 1
+TAIL_CHAINS = [1, 3]
+TAIL_V_EVAC = False
+TAIL_V_PARITY = 1
+TAIL_SYNC_STORES = True
+EVAC_PER_STEP = 2
+SMALL_DELAY = 1
+
+
+def share(width, frac):
+    return min(width - 8, max(8, int(round(width * frac / 8.0)) * 8))
 
 
 def make_pieces():
     pieces = []
     for b, (b0, bw) in enumerate(BLOCKS):
-        for c in range(PASSES):
-            widths = [bw]
-            if b == 0 and c == 0:
-                widths = HEAD_WIDTHS
-            if b == len(BLOCKS) - 1 and c == PASSES - 1:
-                widths = TAIL_WIDTHS
+        last_block = b == len(BLOCKS) - 1
+        n_whole = PASSES - TAIL_PASSES if last_block else PASSES
+        for c in range(n_whole):
+            widths = HEAD_WIDTHS if (b == 0 and c == 0) else [bw]
             off = b0
             for w in widths:
                 pieces.append({"b": b, "c": c, "e0": off, "w": w, "last_in_pass": off + w == b0 + bw})
                 off += w
+        if last_block:
+            off = b0
+            slices = []
+            for w in TAIL_WIDTHS:
+                slices.append((off, w))
+                off += w
+            i0 = 0
+            for n in TAIL_CHAINS:
+                group = slices[i0 : i0 + n]
+                for i, (e0, w) in enumerate(group):
+                    for c in range(n_whole, PASSES):
+                        pieces.append(
+                            {
+                                "b": b, "c": c, "e0": e0, "w": w, "last_in_pass": False,
+                                "chain_first": i == 0 and c == n_whole,
+                                "chain_last": i == n - 1 and c == PASSES - 1,
+                                "chain_e0": group[0][0],
+                            }
+                        )
+                i0 += n
     return pieces
 
 
@@ -62,12 +95,27 @@ def make_units(pieces):
     return units
 
 
+def make_groups():
+    where = {}
+    gid = 0
+    for b, (b0, bw) in enumerate(BLOCKS):
+        off = b0
+        for gw in GROUPS[b]:
+            for i in range(gw // P):
+                where[off // P + i] = (gid, i, gw // P)
+            off += gw
+            gid += 1
+    return where
+
+
 def tile_v2emsgpass_kernel(tc, X, H, out):
     nc = tc.nc
     pieces = make_pieces()
     units = make_units(pieces)
+    where = make_groups()
     n_units = len(units)
     h_view = H.rearrange("(c p j) e -> c p j e", p=P, j=PACK)
+    two_phase = [b == len(BLOCKS) - 1 for b in range(len(BLOCKS))]
 
     with ExitStack() as ctx:
         ctx.enter_context(tc.manual_schedule())
@@ -76,7 +124,7 @@ def tile_v2emsgpass_kernel(tc, X, H, out):
         grp_pool = ctx.enter_context(tc.tile_pool(name="grpp", bufs=GRP_BUFS))
         code_pool = ctx.enter_context(tc.tile_pool(name="codep", bufs=CODE_BUFS))
         out_pool = ctx.enter_context(tc.tile_pool(name="outp", bufs=OUT_BUFS))
-        mx_psum = ctx.enter_context(tc.psum_pool(name="mxps", bufs=6))
+        mx_psum = ctx.enter_context(tc.psum_pool(name="mxps", bufs=MX_BANKS))
         deg_psum = ctx.enter_context(tc.psum_pool(name="degps", bufs=2))
 
         ones = const.tile([P, NDEG], BF16, name="ones")
@@ -89,44 +137,73 @@ def tile_v2emsgpass_kernel(tc, X, H, out):
         inv = const.tile([P, n_tiles], F32, name="inv")
 
         raw_tiles = {}
+        state = {"next_load": 0, "step": 0, "next_deg": 0, "deg_unit": 0, "tail_evacs": 0, "loads_done": False}
 
-        def load(k):
+        held = []
+
+        def flush_held():
+            while held and state["loads_done"]:
+                held.pop(0)()
+
+        def load_next():
+            k = state["next_load"]
+            if k >= len(pieces):
+                return
+            state["next_load"] = k + 1
             pc = pieces[k]
             raw = raw_pool.tile([P, PACK, pc["w"]], BF16, name="raw", tag="raw")
             nc.sync.dma_start(out=raw[:], in_=h_view[pc["c"], :, :, pc["e0"] : pc["e0"] + pc["w"]])
             raw_tiles[k] = raw
+            state["loads_done"] = k + 1 == len(pieces)
+            flush_held()
 
         x_raw = const.tile([P, PASSES, PACK, D], BF16, name="x_raw")
-        nc.sync.dma_start(out=x_raw[:], in_=X.rearrange("(c p j) d -> p c j d", p=P, j=PACK))
-        for k in range(RAW_BUFS):
-            load(k)
         x_grp = const.tile([P, PASSES, D, PACK], BF16, name="x_grp", align_bytes=64)
-        nc.vector.tensor_copy(
-            out=x_grp[:, :X_V_PASSES], in_=x_raw[:, :X_V_PASSES].rearrange("p c j d -> p c d j")
-        )
-        nc.scalar.copy(out=x_grp[:, X_V_PASSES:], in_=x_raw[:, X_V_PASSES:].rearrange("p c j d -> p c d j"))
         x_codes = const.tile([P, PASSES, D], U32, name="x_codes", align_bytes=64)
         x_scales = const.tile([P, PASSES, D], U8, name="x_scales", align_bytes=64)
-        nc.vector.quantize_mx(
-            out=x_codes[:].rearrange("p c d -> p (c d)").bitcast(FP8X4),
-            scales=x_scales[:].rearrange("p c d -> p (c d)"),
-            in_=x_grp[:].rearrange("p c d j -> p (c d j)"),
-        )
+
+        for k in range(X_AFTER):
+            load_next()
+        nc.sync.dma_start(out=x_raw[:], in_=X.rearrange("(c p j) d -> p c j d", p=P, j=PACK))
+        for k in range(RAW_BUFS - X_AFTER):
+            load_next()
+
+        def prepare_x():
+            nc.vector.tensor_copy(
+                out=x_grp[:, :X_V_PASSES], in_=x_raw[:, :X_V_PASSES].rearrange("p c j d -> p c d j")
+            )
+            nc.scalar.copy(out=x_grp[:, X_V_PASSES:], in_=x_raw[:, X_V_PASSES:].rearrange("p c j d -> p c d j"))
+            nc.vector.quantize_mx(
+                out=x_codes[:].rearrange("p c d -> p (c d)").bitcast(FP8X4),
+                scales=x_scales[:].rearrange("p c d -> p (c d)"),
+                in_=x_grp[:].rearrange("p c d j -> p (c d j)"),
+            )
 
         deg_tiles = {}
         banks = {}
         grp_tiles = {}
+        small = []
+        ready = []
+        chain_left = {}
+
+        def pop_small():
+            if small and small[0][0] <= state["step"]:
+                small.pop(0)[1]()
+
+        def push_small(fn):
+            small.append((max(state["step"], state["deg_unit"]) + SMALL_DELAY, fn))
 
         def degree_matmuls(k):
             pc = pieces[k]
             b, c = pc["b"], pc["c"]
             b0, bw = BLOCKS[b]
-            phase = 1 if c == PASSES - 1 else 0
+            phase = 1 if (two_phase[b] and c >= PASSES - TAIL_PASSES) else 0
             if (b, phase) not in deg_tiles:
                 deg_tiles[(b, phase)] = deg_psum.tile([P, bw // P, NDEG], F32, name="deg", tag="deg")
             dt_ = deg_tiles[(b, phase)]
             raw = raw_tiles[k]
             n_t = pc["w"] // P
+            last_c = PASSES - TAIL_PASSES - 1 if two_phase[b] else PASSES - 1
             for t in range(n_t):
                 lt = (pc["e0"] - b0) // P + t
                 for j in range(PACK):
@@ -134,26 +211,50 @@ def tile_v2emsgpass_kernel(tc, X, H, out):
                     final = t == n_t - 1 and j == PACK - 1
                     if phase == 0:
                         start = first and c == 0 and pc["e0"] == b0
-                        stop = final and c == PASSES - 2 and pc["last_in_pass"]
+                        stop = final and c == last_c and pc["last_in_pass"]
                     else:
-                        start = first
-                        stop = final
+                        start = first and pc["chain_first"]
+                        stop = final and pc["chain_last"]
                     nc.tensor.matmul(
-                        out=dt_[:, lt, :],
-                        lhsT=raw[:, j, t * P : (t + 1) * P],
-                        rhs=ones[:],
-                        start=start,
-                        stop=stop,
+                        out=dt_[:, lt, :], lhsT=raw[:, j, t * P : (t + 1) * P], rhs=ones[:], start=start, stop=stop
                     )
+            ta, tb = pc.get("chain_e0", pc["e0"]) // P, (pc["e0"] + pc["w"]) // P
+            la, lb = ta - b0 // P, tb - b0 // P
+            if two_phase[b] and c == last_c and pc["last_in_pass"]:
+                push_small(lambda: nc.vector.tensor_copy(out=d1[:, b0 // P : (b0 + bw) // P], in_=dt_[:, :, 0]))
+            if c == PASSES - 1 and pc.get("chain_last", True):
+                if two_phase[b]:
+                    push_small(
+                        lambda: nc.vector.tensor_tensor(
+                            out=dg[:, ta:tb], in0=dt_[:, la:lb, 0], in1=d1[:, ta:tb], op=ALU.add
+                        )
+                    )
+                else:
+                    push_small(lambda: nc.vector.tensor_copy(out=dg[:, ta:tb], in_=dt_[:, la:lb, 0]))
+                push_small(
+                    lambda: nc.vector.scalar_tensor_tensor(
+                        out=sf[:, ta:tb], in0=dg[:, ta:tb], scalar=0.0, in1=dg[:, ta:tb],
+                        op0=ALU.is_equal, op1=ALU.add,
+                    )
+                )
+                push_small(lambda: nc.vector.reciprocal(out=rc[:, ta:tb], in_=sf[:, ta:tb]))
 
-        def regroup(s):
+                def last_op():
+                    nc.vector.scalar_tensor_tensor(
+                        out=inv[:, ta:tb], in0=dg[:, ta:tb], scalar=0.0, in1=rc[:, ta:tb],
+                        op0=ALU.not_equal, op1=ALU.mult,
+                    )
+                    for te in range(ta, tb):
+                        chain_left[where[te][0]] = False
+
+                push_small(last_op)
+
+        def regroup(s, frac):
             u = units[s]
             k = u["k"]
-            if u["first"]:
-                degree_matmuls(k)
             raw = raw_tiles[k]
             w = u["w"]
-            cv = V_SHARE_LAST if s == n_units - 1 else V_SHARE[w]
+            cv = share(w, frac)
             g = grp_pool.tile([P, w, PACK], BF16, name="grp", tag="grp", align_bytes=64)
             o = u["off"]
             nc.vector.tensor_copy(
@@ -165,14 +266,13 @@ def tile_v2emsgpass_kernel(tc, X, H, out):
                 in_=raw[:, :, o + cv : o + w].rearrange("p t (c i) -> p c t i", i=4),
             )
             grp_tiles[s] = g
-            if u["last"] and k + RAW_BUFS < len(pieces):
-                load(k + RAW_BUFS)
+            if u["last"]:
+                load_next()
 
         def quantise_and_multiply(s):
             u = units[s]
             pc = pieces[u["k"]]
-            b, c = pc["b"], pc["c"]
-            b0, bw = BLOCKS[b]
+            c = pc["c"]
             w = u["w"]
             g = grp_tiles[s]
             codes = code_pool.tile([P, w], U32, name="codes", tag="codes", align_bytes=64)
@@ -181,66 +281,90 @@ def tile_v2emsgpass_kernel(tc, X, H, out):
                 out=codes[:].bitcast(FP8X4), scales=scales[:], in_=g[:].rearrange("p w j -> p (w j)")
             )
             e0 = pc["e0"] + u["off"]
-            closed = []
             for t in range(w // P):
                 te = e0 // P + t
-                bank_id = te // TILES_PER_BANK
-                slot = te % TILES_PER_BANK
+                gid, slot, n_slots = where[te]
                 if c == 0 and slot == 0:
-                    banks[bank_id] = mx_psum.tile([P, BANK_COLS], F32, name="acc", tag="acc")
+                    banks[gid] = mx_psum.tile([P, n_slots * P], F32, name="acc", tag="acc")
+                    chain_left[gid] = True
                 nc.tensor.matmul_mx(
-                    out=banks[bank_id][:, slot * P : (slot + 1) * P],
+                    out=banks[gid][:, slot * P : (slot + 1) * P],
                     lhsT=codes[:, t * P : (t + 1) * P].bitcast(FP8X4),
                     lhsT_scale=scales[:, t * P : (t + 1) * P],
                     rhs=x_codes[:, c, :].bitcast(FP8X4),
                     rhs_scale=x_scales[:, c, :],
                     start=(c == 0 and slot == 0),
-                    stop=(c == PASSES - 1 and slot == TILES_PER_BANK - 1),
+                    stop=(c == PASSES - 1 and slot == n_slots - 1),
                 )
-                if c == PASSES - 1 and slot == TILES_PER_BANK - 1:
-                    closed.append(bank_id)
-            if c == PASSES - 2 and pc["last_in_pass"] and u["last"]:
-                ta, tb = b0 // P, (b0 + bw) // P
-                nc.vector.tensor_copy(out=d1[:, ta:tb], in_=deg_tiles[(b, 0)][:, :, 0])
-            if c == PASSES - 1 and u["first"]:
-                ta, tb = pc["e0"] // P, (pc["e0"] + pc["w"]) // P
-                la, lb = ta - b0 // P, tb - b0 // P
+                if c == PASSES - 1 and slot == n_slots - 1:
+                    ready.append((gid, te - slot, n_slots))
+
+        def evacuate(gid, te0, n_slots):
+            acc = banks[gid]
+            res = out_pool.tile([P, n_slots, D], F32, name="res", tag="res")
+            in_tail = te0 * P >= BLOCKS[-1][0]
+            on_vector = in_tail and TAIL_V_EVAC and state["tail_evacs"] % 2 == TAIL_V_PARITY
+            if in_tail:
+                state["tail_evacs"] += 1
+            if on_vector:
                 nc.vector.tensor_tensor(
-                    out=dg[:, ta:tb], in0=deg_tiles[(b, 1)][:, la:lb, 0], in1=d1[:, ta:tb], op=ALU.add
+                    out=res[:],
+                    in0=acc[:].rearrange("p (s d) -> p s d", d=D),
+                    in1=inv[:, te0 : te0 + n_slots].unsqueeze(2).to_broadcast([P, n_slots, D]),
+                    op=ALU.mult,
                 )
-                nc.vector.scalar_tensor_tensor(
-                    out=sf[:, ta:tb], in0=dg[:, ta:tb], scalar=0.0, in1=dg[:, ta:tb],
-                    op0=ALU.is_equal, op1=ALU.add,
-                )
-                nc.vector.reciprocal(out=rc[:, ta:tb], in_=sf[:, ta:tb])
-                nc.vector.scalar_tensor_tensor(
-                    out=inv[:, ta:tb], in0=dg[:, ta:tb], scalar=0.0, in1=rc[:, ta:tb],
-                    op0=ALU.not_equal, op1=ALU.mult,
-                )
-            return closed
+            else:
+                for slot in range(n_slots):
+                    nc.scalar.activation(
+                        out=res[:, slot, :],
+                        in_=acc[:, slot * P : (slot + 1) * P],
+                        func=ACT.Copy,
+                        scale=inv[:, te0 + slot : te0 + slot + 1],
+                    )
+            e0 = te0 * P
+            dst = out[e0 : e0 + n_slots * P, :].rearrange("(s p) d -> p s d", p=P)
+            if in_tail:
+                queue = nc.sync if TAIL_SYNC_STORES else nc.scalar
+                queue.dma_start(out=dst, in_=res[:])
+            elif DEFER_STORES:
+                held.append(lambda: nc.sync.dma_start(out=dst, in_=res[:]))
+                flush_held()
+            else:
+                nc.scalar.dma_start(out=dst, in_=res[:])
 
-        def evacuate(bank_id):
-            acc = banks[bank_id]
-            res = out_pool.tile([P, TILES_PER_BANK, D], F32, name="res", tag="res")
-            for slot in range(TILES_PER_BANK):
-                te = bank_id * TILES_PER_BANK + slot
-                nc.scalar.activation(
-                    out=res[:, slot, :],
-                    in_=acc[:, slot * P : (slot + 1) * P],
-                    func=ACT.Copy,
-                    scale=inv[:, te : te + 1],
-                )
-            e0 = bank_id * BANK_COLS
-            nc.scalar.dma_start(
-                out=out[e0 : e0 + BANK_COLS, :].rearrange("(s p) d -> p s d", p=P), in_=res[:]
-            )
+        first_unit = {}
+        for i, u in enumerate(units):
+            if u["first"]:
+                first_unit[u["k"]] = i
 
-        closed_prev = []
-        for s in range(n_units + 2):
+        def degrees_up_to(step):
+            while state["next_deg"] < len(pieces) and first_unit[state["next_deg"]] <= step + DEG_AHEAD:
+                if state["next_deg"] not in raw_tiles:
+                    break
+                state["deg_unit"] = first_unit[state["next_deg"]]
+                degree_matmuls(state["next_deg"])
+                state["next_deg"] += 1
+
+        s = 0
+        while s < n_units + 1 or ready or small:
+            state["step"] = s
+            if s == 0:
+                degrees_up_to(-DEG_AHEAD)
+            will_evac = bool(ready) and not chain_left[ready[0][0]]
             if s < n_units:
-                regroup(s)
-            for bank_id in closed_prev:
-                evacuate(bank_id)
-            closed_prev = []
+                frac = V_FRAC_EVAC if will_evac else V_FRAC
+                if s >= n_units - len(V_FRAC_TAIL):
+                    frac = V_FRAC_TAIL[s - (n_units - len(V_FRAC_TAIL))]
+                regroup(s, frac)
+                if s == X_AFTER - 1 or (X_AFTER == 0 and s == 0):
+                    prepare_x()
+            pop_small()
+            n_evac = 0
+            while ready and not chain_left[ready[0][0]] and (n_evac < EVAC_PER_STEP or s >= n_units):
+                evacuate(*ready.pop(0))
+                n_evac += 1
             if 1 <= s <= n_units:
-                closed_prev = quantise_and_multiply(s - 1)
+                quantise_and_multiply(s - 1)
+            degrees_up_to(s + 1)
+            pop_small()
+            s += 1

@@ -26,7 +26,7 @@ BLOCKS = [(0, 2048), (2048, 2048)]
 HEAD_WIDTHS = [512, 512, 1024]
 TAIL_WIDTHS = [1024, 512, 256, 256]
 GROUPS = [[512, 512, 512, 512], [512, 512, 512, 256, 256]]
-RAW_BUFS = 6
+RAW_BUFS = 7
 GRP_BUFS = 4
 CODE_BUFS = 6
 OUT_BUFS = 8
@@ -36,6 +36,7 @@ V_FRAC_EVAC = 0.7
 V_FRAC_TAIL = [0.4, 0.4, 0.4, 0.45]
 X_V_PASSES = 6
 X_AFTER = 1
+DEG_RUN = 8
 DEG_AHEAD = 1
 DEFER_STORES = True
 TAIL_PASSES = 1
@@ -129,6 +130,9 @@ def tile_v2emsgpass_kernel(tc, X, H, out):
 
         ones = const.tile([P, NDEG], BF16, name="ones")
         nc.vector.memset(ones[:], 1.0)
+        warm = const.tile([P, 2], F32, name="warm")
+        nc.vector.memset(warm[:, 0:1], 1.0)
+        nc.scalar.activation(out=warm[:, 1:2], in_=warm[:, 0:1], func=ACT.Copy)
         n_tiles = N_EDGE // P
         d1 = const.tile([P, n_tiles], F32, name="d1")
         dg = const.tile([P, n_tiles], F32, name="dg")
@@ -137,7 +141,7 @@ def tile_v2emsgpass_kernel(tc, X, H, out):
         inv = const.tile([P, n_tiles], F32, name="inv")
 
         raw_tiles = {}
-        state = {"next_load": 0, "step": 0, "next_deg": 0, "deg_unit": 0, "tail_evacs": 0, "loads_done": False}
+        state = {"next_load": 0, "step": 0, "next_deg": 0, "deg_unit": 0, "tail_evacs": 0, "loads_done": False, "deg_tile": 0}
 
         held = []
 
@@ -193,7 +197,7 @@ def tile_v2emsgpass_kernel(tc, X, H, out):
         def push_small(fn):
             small.append((max(state["step"], state["deg_unit"]) + SMALL_DELAY, fn))
 
-        def degree_matmuls(k):
+        def degree_matmuls(k, t_lo, t_hi):
             pc = pieces[k]
             b, c = pc["b"], pc["c"]
             b0, bw = BLOCKS[b]
@@ -204,7 +208,7 @@ def tile_v2emsgpass_kernel(tc, X, H, out):
             raw = raw_tiles[k]
             n_t = pc["w"] // P
             last_c = PASSES - TAIL_PASSES - 1 if two_phase[b] else PASSES - 1
-            for t in range(n_t):
+            for t in range(t_lo, t_hi):
                 lt = (pc["e0"] - b0) // P + t
                 for j in range(PACK):
                     first = t == 0 and j == 0
@@ -218,6 +222,8 @@ def tile_v2emsgpass_kernel(tc, X, H, out):
                     nc.tensor.matmul(
                         out=dt_[:, lt, :], lhsT=raw[:, j, t * P : (t + 1) * P], rhs=ones[:], start=start, stop=stop
                     )
+            if t_hi < n_t:
+                return
             ta, tb = pc.get("chain_e0", pc["e0"]) // P, (pc["e0"] + pc["w"]) // P
             la, lb = ta - b0 // P, tb - b0 // P
             if two_phase[b] and c == last_c and pc["last_in_pass"]:
@@ -338,12 +344,19 @@ def tile_v2emsgpass_kernel(tc, X, H, out):
                 first_unit[u["k"]] = i
 
         def degrees_up_to(step):
-            while state["next_deg"] < len(pieces) and first_unit[state["next_deg"]] <= step + DEG_AHEAD:
-                if state["next_deg"] not in raw_tiles:
+            while state["next_deg"] < len(pieces):
+                k = state["next_deg"]
+                t_lo = state["deg_tile"]
+                if k not in raw_tiles or first_unit[k] + t_lo // DEG_RUN > step + DEG_AHEAD:
                     break
-                state["deg_unit"] = first_unit[state["next_deg"]]
-                degree_matmuls(state["next_deg"])
-                state["next_deg"] += 1
+                n_t = pieces[k]["w"] // P
+                t_hi = min(n_t, t_lo + DEG_RUN)
+                state["deg_unit"] = first_unit[k]
+                degree_matmuls(k, t_lo, t_hi)
+                state["deg_tile"] = t_hi
+                if t_hi == n_t:
+                    state["next_deg"] = k + 1
+                    state["deg_tile"] = 0
 
         s = 0
         while s < n_units + 1 or ready or small:

@@ -31,7 +31,7 @@ GRP_BUFS = 4
 CODE_BUFS = 6
 OUT_BUFS = 8
 MX_BANKS = 6
-V_FRAC = 0.49
+V_FRAC = 0.47
 V_FRAC_EVAC = 0.7
 V_FRAC_TAIL = [0.4, 0.4, 0.4, 0.45]
 X_V_PASSES = 6

@@ -119,7 +119,6 @@ def tile_v2emsgpass_kernel(tc, X, H, out):
     two_phase = [b == len(BLOCKS) - 1 for b in range(len(BLOCKS))]
 
     with ExitStack() as ctx:
-        ctx.enter_context(tc.manual_schedule())
         const = ctx.enter_context(tc.tile_pool(name="const", bufs=1))
         raw_pool = ctx.enter_context(tc.tile_pool(name="rawp", bufs=RAW_BUFS))
         grp_pool = ctx.enter_context(tc.tile_pool(name="grpp", bufs=GRP_BUFS))

@@ -267,8 +267,8 @@ def tile_v2emsgpass_kernel(tc, X, H, out):
                 in_=raw[:, :, o : o + cv].rearrange("p t (c i) -> p c t i", i=4),
             )
             nc.scalar.copy(
-                out=g[:, cv:w, :].rearrange("p (c i) t -> p c t i", i=4),
-                in_=raw[:, :, o + cv : o + w].rearrange("p t (c i) -> p c t i", i=4),
+                out=g[:, cv:w, :].rearrange("p (c i) t -> p c t i", i=8),
+                in_=raw[:, :, o + cv : o + w].rearrange("p t (c i) -> p c t i", i=8),
             )
             grp_tiles[s] = g
             if u["last"]:

@@ -23,7 +23,7 @@ NDEG = 12
 FLOPS = 2 * N_VERT * N_EDGE * D
 
 BLOCKS = [(0, 2048), (2048, 2048)]
-HEAD_WIDTHS = [512, 512, 1024]
+HEAD_WIDTHS = [2048]
 TAIL_WIDTHS = [1024, 512, 256, 256]
 GROUPS = [[512, 512, 512, 512], [512, 512, 512, 256, 256]]
 RAW_BUFS = 7

@@ -24,7 +24,8 @@ FLOPS = 2 * N_VERT * N_EDGE * D
 
 BLOCKS = [(0, 2048), (2048, 2048)]
 HEAD_WIDTHS = [2048]
-TAIL_WIDTHS = [1024, 512, 256, 256]
+TAIL_WIDTHS = [1024, 1024]
+LAST_UNITS = [512, 256, 256]
 GROUPS = [[512, 512, 512, 512], [512, 512, 512, 256, 256]]
 RAW_BUFS = 7
 GRP_BUFS = 4
@@ -39,8 +40,8 @@ X_AFTER = 1
 DEG_RUN = 8
 DEG_AHEAD = 1
 DEFER_STORES = True
-TAIL_PASSES = 1
-TAIL_CHAINS = [1, 3]
+TAIL_PASSES = 2
+TAIL_CHAINS = [1, 1]
 TAIL_V_EVAC = False
 TAIL_V_PARITY = 1
 TAIL_SYNC_STORES = True
@@ -89,10 +90,11 @@ def make_pieces():
 def make_units(pieces):
     units = []
     for k, pc in enumerate(pieces):
-        n_u = max(1, pc["w"] // UNIT)
-        uw = pc["w"] // n_u
-        for i in range(n_u):
-            units.append({"k": k, "off": i * uw, "w": uw, "first": i == 0, "last": i == n_u - 1})
+        widths = LAST_UNITS if k == len(pieces) - 1 else [min(UNIT, pc["w"])] * max(1, pc["w"] // UNIT)
+        off = 0
+        for i, uw in enumerate(widths):
+            units.append({"k": k, "off": off, "w": uw, "first": i == 0, "last": i == len(widths) - 1})
+            off += uw
     return units
 
 
@@ -201,9 +203,10 @@ def tile_v2emsgpass_kernel(tc, X, H, out):
             b, c = pc["b"], pc["c"]
             b0, bw = BLOCKS[b]
             phase = 1 if (two_phase[b] and c >= PASSES - TAIL_PASSES) else 0
-            if (b, phase) not in deg_tiles:
-                deg_tiles[(b, phase)] = deg_psum.tile([P, bw // P, NDEG], F32, name="deg", tag="deg")
-            dt_ = deg_tiles[(b, phase)]
+            span = (b, phase, pc.get("chain_e0", 0))
+            if span not in deg_tiles:
+                deg_tiles[span] = deg_psum.tile([P, bw // P, NDEG], F32, name="deg", tag="deg")
+            dt_ = deg_tiles[span]
             raw = raw_tiles[k]
             n_t = pc["w"] // P
             last_c = PASSES - TAIL_PASSES - 1 if two_phase[b] else PASSES - 1

@@ -50,7 +50,7 @@ SMALL_DELAY = 1
 
 
 def share(width, frac):
-    return min(width - 8, max(8, int(round(width * frac / 8.0)) * 8))
+    return min(width - 16, max(16, int(round(width * frac / 16.0)) * 16))
 
 
 def make_pieces():
@@ -266,8 +266,8 @@ def tile_v2emsgpass_kernel(tc, X, H, out):
             g = grp_pool.tile([P, w, PACK], BF16, name="grp", tag="grp", align_bytes=64)
             o = u["off"]
             nc.vector.tensor_copy(
-                out=g[:, 0:cv, :].rearrange("p (c i) t -> p c t i", i=4),
-                in_=raw[:, :, o : o + cv].rearrange("p t (c i) -> p c t i", i=4),
+                out=g[:, 0:cv, :].rearrange("p (c i) t -> p c t i", i=8),
+                in_=raw[:, :, o : o + cv].rearrange("p t (c i) -> p c t i", i=8),
             )
             nc.scalar.copy(
                 out=g[:, cv:w, :].rearrange("p (c i) t -> p c t i", i=8),

@@ -32,7 +32,7 @@ GRP_BUFS = 4
 CODE_BUFS = 6
 OUT_BUFS = 8
 MX_BANKS = 6
-V_FRAC = 0.47
+V_FRAC = 0.485
 V_FRAC_EVAC = 0.7
 V_FRAC_TAIL = [0.4, 0.4, 0.4, 0.45]
 X_V_PASSES = 6

@@ -33,7 +33,7 @@ CODE_BUFS = 6
 OUT_BUFS = 8
 MX_BANKS = 6
 V_FRAC = 0.485
-V_FRAC_EVAC = 0.7
+V_FRAC_EVAC = 0.65
 V_FRAC_TAIL = [0.4, 0.4, 0.4, 0.45]
 X_V_PASSES = 6
 X_AFTER = 1

from contextlib import ExitStack

import concourse.mybir as mybir

BF16 = mybir.dt.bfloat16
F32 = mybir.dt.float32
U32 = mybir.dt.uint32
U8 = mybir.dt.uint8
FP8X4 = mybir.dt.float8_e4m3fn_x4
ALU = mybir.AluOpType
ACT = mybir.ActivationFunctionType

P = 128
PACK = 4
K_PASS = P * PACK
N_VERT = 4096
N_EDGE = 4096
D = 128
PASSES = N_VERT // K_PASS
UNIT = 1024
NDEG = 12

FLOPS = 2 * N_VERT * N_EDGE * D

BLOCKS = [(0, 2048), (2048, 2048)]
HEAD_WIDTHS = [2048]
TAIL_WIDTHS = [1024, 1024]
LAST_UNITS = [512, 256, 256]
GROUPS = [[512, 512, 512, 512], [512, 512, 512, 256, 256]]
RAW_BUFS = 7
GRP_BUFS = 4
CODE_BUFS = 6
OUT_BUFS = 8
MX_BANKS = 6
V_FRAC = 0.485
V_FRAC_EVAC = 0.65
V_FRAC_TAIL = [0.4, 0.4, 0.4, 0.45]
X_V_PASSES = 6
X_AFTER = 1
DEG_RUN = 8
DEG_AHEAD = 1
DEFER_STORES = True
TAIL_PASSES = 2
TAIL_CHAINS = [1, 1]
TAIL_V_EVAC = False
TAIL_V_PARITY = 1
TAIL_SYNC_STORES = True
EVAC_PER_STEP = 2
SMALL_DELAY = 1


def share(width, frac):
    return min(width - 16, max(16, int(round(width * frac / 16.0)) * 16))


def make_pieces():
    pieces = []
    for b, (b0, bw) in enumerate(BLOCKS):
        last_block = b == len(BLOCKS) - 1
        n_whole = PASSES - TAIL_PASSES if last_block else PASSES
        for c in range(n_whole):
            widths = HEAD_WIDTHS if (b == 0 and c == 0) else [bw]
            off = b0
            for w in widths:
                pieces.append({"b": b, "c": c, "e0": off, "w": w, "last_in_pass": off + w == b0 + bw})
                off += w
        if last_block:
            off = b0
            slices = []
            for w in TAIL_WIDTHS:
                slices.append((off, w))
                off += w
            i0 = 0
            for n in TAIL_CHAINS:
                group = slices[i0 : i0 + n]
                for i, (e0, w) in enumerate(group):
                    for c in range(n_whole, PASSES):
                        pieces.append(
                            {
                                "b": b, "c": c, "e0": e0, "w": w, "last_in_pass": False,
                                "chain_first": i == 0 and c == n_whole,
                                "chain_last": i == n - 1 and c == PASSES - 1,
                                "chain_e0": group[0][0],
                            }
                        )
                i0 += n
    return pieces


def make_units(pieces):
    units = []
    for k, pc in enumerate(pieces):
        widths = LAST_UNITS if k == len(pieces) - 1 else [min(UNIT, pc["w"])] * max(1, pc["w"] // UNIT)
        off = 0
        for i, uw in enumerate(widths):
            units.append({"k": k, "off": off, "w": uw, "first": i == 0, "last": i == len(widths) - 1})
            off += uw
    return units


def make_groups():
    where = {}
    gid = 0
    for b, (b0, bw) in enumerate(BLOCKS):
        off = b0
        for gw in GROUPS[b]:
            for i in range(gw // P):
                where[off // P + i] = (gid, i, gw // P)
            off += gw
            gid += 1
    return where


def tile_v2emsgpass_kernel(tc, X, H, out):
    nc = tc.nc
    pieces = make_pieces()
    units = make_units(pieces)
    where = make_groups()
    n_units = len(units)
    h_view = H.rearrange("(c p j) e -> c p j e", p=P, j=PACK)
    two_phase = [b == len(BLOCKS) - 1 for b in range(len(BLOCKS))]

    with ExitStack() as ctx:
        const = ctx.enter_context(tc.tile_pool(name="const", bufs=1))
        raw_pool = ctx.enter_context(tc.tile_pool(name="rawp", bufs=RAW_BUFS))
        grp_pool = ctx.enter_context(tc.tile_pool(name="grpp", bufs=GRP_BUFS))
        code_pool = ctx.enter_context(tc.tile_pool(name="codep", bufs=CODE_BUFS))
        out_pool = ctx.enter_context(tc.tile_pool(name="outp", bufs=OUT_BUFS))
        mx_psum = ctx.enter_context(tc.psum_pool(name="mxps", bufs=MX_BANKS))
        deg_psum = ctx.enter_context(tc.psum_pool(name="degps", bufs=2))

        ones = const.tile([P, NDEG], BF16, name="ones")
        nc.vector.memset(ones[:], 1.0)
        warm = const.tile([P, 2], F32, name="warm")
        nc.vector.memset(warm[:, 0:1], 1.0)
        nc.scalar.activation(out=warm[:, 1:2], in_=warm[:, 0:1], func=ACT.Copy)
        n_tiles = N_EDGE // P
        d1 = const.tile([P, n_tiles], F32, name="d1")
        dg = const.tile([P, n_tiles], F32, name="dg")
        sf = const.tile([P, n_tiles], F32, name="sf")
        rc = const.tile([P, n_tiles], F32, name="rc")
        inv = const.tile([P, n_tiles], F32, name="inv")

        raw_tiles = {}
        state = {"next_load": 0, "step": 0, "next_deg": 0, "deg_unit": 0, "tail_evacs": 0, "loads_done": False, "deg_tile": 0}

        held = []

        def flush_held():
            while held and state["loads_done"]:
                held.pop(0)()

        def load_next():
            k = state["next_load"]
            if k >= len(pieces):
                return
            state["next_load"] = k + 1
            pc = pieces[k]
            raw = raw_pool.tile([P, PACK, pc["w"]], BF16, name="raw", tag="raw")
            nc.sync.dma_start(out=raw[:], in_=h_view[pc["c"], :, :, pc["e0"] : pc["e0"] + pc["w"]])
            raw_tiles[k] = raw
            state["loads_done"] = k + 1 == len(pieces)
            flush_held()

        x_raw = const.tile([P, PASSES, PACK, D], BF16, name="x_raw")
        x_grp = const.tile([P, PASSES, D, PACK], BF16, name="x_grp", align_bytes=64)
        x_codes = const.tile([P, PASSES, D], U32, name="x_codes", align_bytes=64)
        x_scales = const.tile([P, PASSES, D], U8, name="x_scales", align_bytes=64)

        for k in range(X_AFTER):
            load_next()
        nc.sync.dma_start(out=x_raw[:], in_=X.rearrange("(c p j) d -> p c j d", p=P, j=PACK))
        for k in range(RAW_BUFS - X_AFTER):
            load_next()

        def prepare_x():
            nc.vector.tensor_copy(
                out=x_grp[:, :X_V_PASSES], in_=x_raw[:, :X_V_PASSES].rearrange("p c j d -> p c d j")
            )
            nc.scalar.copy(out=x_grp[:, X_V_PASSES:], in_=x_raw[:, X_V_PASSES:].rearrange("p c j d -> p c d j"))
            nc.vector.quantize_mx(
                out=x_codes[:].rearrange("p c d -> p (c d)").bitcast(FP8X4),
                scales=x_scales[:].rearrange("p c d -> p (c d)"),
                in_=x_grp[:].rearrange("p c d j -> p (c d j)"),
            )

        deg_tiles = {}
        banks = {}
        grp_tiles = {}
        small = []
        ready = []
        chain_left = {}

        def pop_small():
            if small and small[0][0] <= state["step"]:
                small.pop(0)[1]()

        def push_small(fn):
            small.append((max(state["step"], state["deg_unit"]) + SMALL_DELAY, fn))

        def degree_matmuls(k, t_lo, t_hi):
            pc = pieces[k]
            b, c = pc["b"], pc["c"]
            b0, bw = BLOCKS[b]
            phase = 1 if (two_phase[b] and c >= PASSES - TAIL_PASSES) else 0
            span = (b, phase, pc.get("chain_e0", 0))
            if span not in deg_tiles:
                deg_tiles[span] = deg_psum.tile([P, bw // P, NDEG], F32, name="deg", tag="deg")
            dt_ = deg_tiles[span]
            raw = raw_tiles[k]
            n_t = pc["w"] // P
            last_c = PASSES - TAIL_PASSES - 1 if two_phase[b] else PASSES - 1
            for t in range(t_lo, t_hi):
                lt = (pc["e0"] - b0) // P + t
                for j in range(PACK):
                    first = t == 0 and j == 0
                    final = t == n_t - 1 and j == PACK - 1
                    if phase == 0:
                        start = first and c == 0 and pc["e0"] == b0
                        stop = final and c == last_c and pc["last_in_pass"]
                    else:
                        start = first and pc["chain_first"]
                        stop = final and pc["chain_last"]
                    nc.tensor.matmul(
                        out=dt_[:, lt, :], lhsT=raw[:, j, t * P : (t + 1) * P], rhs=ones[:], start=start, stop=stop
                    )
            if t_hi < n_t:
                return
            ta, tb = pc.get("chain_e0", pc["e0"]) // P, (pc["e0"] + pc["w"]) // P
            la, lb = ta - b0 // P, tb - b0 // P
            if two_phase[b] and c == last_c and pc["last_in_pass"]:
                push_small(lambda: nc.vector.tensor_copy(out=d1[:, b0 // P : (b0 + bw) // P], in_=dt_[:, :, 0]))
            if c == PASSES - 1 and pc.get("chain_last", True):
                if two_phase[b]:
                    push_small(
                        lambda: nc.vector.tensor_tensor(
                            out=dg[:, ta:tb], in0=dt_[:, la:lb, 0], in1=d1[:, ta:tb], op=ALU.add
                        )
                    )
                else:
                    push_small(lambda: nc.vector.tensor_copy(out=dg[:, ta:tb], in_=dt_[:, la:lb, 0]))
                push_small(
                    lambda: nc.vector.scalar_tensor_tensor(
                        out=sf[:, ta:tb], in0=dg[:, ta:tb], scalar=0.0, in1=dg[:, ta:tb],
                        op0=ALU.is_equal, op1=ALU.add,
                    )
                )
                push_small(lambda: nc.vector.reciprocal(out=rc[:, ta:tb], in_=sf[:, ta:tb]))

                def last_op():
                    nc.vector.scalar_tensor_tensor(
                        out=inv[:, ta:tb], in0=dg[:, ta:tb], scalar=0.0, in1=rc[:, ta:tb],
                        op0=ALU.not_equal, op1=ALU.mult,
                    )
                    for te in range(ta, tb):
                        chain_left[where[te][0]] = False

                push_small(last_op)

        def regroup(s, frac):
            u = units[s]
            k = u["k"]
            raw = raw_tiles[k]
            w = u["w"]
            cv = share(w, frac)
            g = grp_pool.tile([P, w, PACK], BF16, name="grp", tag="grp", align_bytes=64)
            o = u["off"]
            nc.vector.tensor_copy(
                out=g[:, 0:cv, :].rearrange("p (c i) t -> p c t i", i=8),
                in_=raw[:, :, o : o + cv].rearrange("p t (c i) -> p c t i", i=8),
            )
            nc.scalar.copy(
                out=g[:, cv:w, :].rearrange("p (c i) t -> p c t i", i=8),
                in_=raw[:, :, o + cv : o + w].rearrange("p t (c i) -> p c t i", i=8),
            )
            grp_tiles[s] = g
            if u["last"]:
                load_next()

        def quantise_and_multiply(s):
            u = units[s]
            pc = pieces[u["k"]]
            c = pc["c"]
            w = u["w"]
            g = grp_tiles[s]
            codes = code_pool.tile([P, w], U32, name="codes", tag="codes", align_bytes=64)
            scales = code_pool.tile([P, w], U8, name="scales", tag="scales", align_bytes=64)
            nc.vector.quantize_mx(
                out=codes[:].bitcast(FP8X4), scales=scales[:], in_=g[:].rearrange("p w j -> p (w j)")
            )
            e0 = pc["e0"] + u["off"]
            for t in range(w // P):
                te = e0 // P + t
                gid, slot, n_slots = where[te]
                if c == 0 and slot == 0:
                    banks[gid] = mx_psum.tile([P, n_slots * P], F32, name="acc", tag="acc")
                    chain_left[gid] = True
                nc.tensor.matmul_mx(
                    out=banks[gid][:, slot * P : (slot + 1) * P],
                    lhsT=codes[:, t * P : (t + 1) * P].bitcast(FP8X4),
                    lhsT_scale=scales[:, t * P : (t + 1) * P],
                    rhs=x_codes[:, c, :].bitcast(FP8X4),
                    rhs_scale=x_scales[:, c, :],
                    start=(c == 0 and slot == 0),
                    stop=(c == PASSES - 1 and slot == n_slots - 1),
                )
                if c == PASSES - 1 and slot == n_slots - 1:
                    ready.append((gid, te - slot, n_slots))

        def evacuate(gid, te0, n_slots):
            acc = banks[gid]
            res = out_pool.tile([P, n_slots, D], F32, name="res", tag="res")
            in_tail = te0 * P >= BLOCKS[-1][0]
            on_vector = in_tail and TAIL_V_EVAC and state["tail_evacs"] % 2 == TAIL_V_PARITY
            if in_tail:
                state["tail_evacs"] += 1
            if on_vector:
                nc.vector.tensor_tensor(
                    out=res[:],
                    in0=acc[:].rearrange("p (s d) -> p s d", d=D),
                    in1=inv[:, te0 : te0 + n_slots].unsqueeze(2).to_broadcast([P, n_slots, D]),
                    op=ALU.mult,
                )
            else:
                for slot in range(n_slots):
                    nc.scalar.activation(
                        out=res[:, slot, :],
                        in_=acc[:, slot * P : (slot + 1) * P],
                        func=ACT.Copy,
                        scale=inv[:, te0 + slot : te0 + slot + 1],
                    )
            e0 = te0 * P
            dst = out[e0 : e0 + n_slots * P, :].rearrange("(s p) d -> p s d", p=P)
            if in_tail:
                queue = nc.sync if TAIL_SYNC_STORES else nc.scalar
                queue.dma_start(out=dst, in_=res[:])
            elif DEFER_STORES:
                held.append(lambda: nc.sync.dma_start(out=dst, in_=res[:]))
                flush_held()
            else:
                nc.scalar.dma_start(out=dst, in_=res[:])

        first_unit = {}
        for i, u in enumerate(units):
            if u["first"]:
                first_unit[u["k"]] = i

        def degrees_up_to(step):
            while state["next_deg"] < len(pieces):
                k = state["next_deg"]
                t_lo = state["deg_tile"]
                if k not in raw_tiles or first_unit[k] + t_lo // DEG_RUN > step + DEG_AHEAD:
                    break
                n_t = pieces[k]["w"] // P
                t_hi = min(n_t, t_lo + DEG_RUN)
                state["deg_unit"] = first_unit[k]
                degree_matmuls(k, t_lo, t_hi)
                state["deg_tile"] = t_hi
                if t_hi == n_t:
                    state["next_deg"] = k + 1
                    state["deg_tile"] = 0

        s = 0
        while s < n_units + 1 or ready or small:
            state["step"] = s
            if s == 0:
                degrees_up_to(-DEG_AHEAD)
            will_evac = bool(ready) and not chain_left[ready[0][0]]
            if s < n_units:
                frac = V_FRAC_EVAC if will_evac else V_FRAC
                if s >= n_units - len(V_FRAC_TAIL):
                    frac = V_FRAC_TAIL[s - (n_units - len(V_FRAC_TAIL))]
                regroup(s, frac)
                if s == X_AFTER - 1 or (X_AFTER == 0 and s == 0):
                    prepare_x()
            pop_small()
            n_evac = 0
            while ready and not chain_left[ready[0][0]] and (n_evac < EVAC_PER_STEP or s >= n_units):
                evacuate(*ready.pop(0))
                n_evac += 1
            if 1 <= s <= n_units:
                quantise_and_multiply(s - 1)
            degrees_up_to(s + 1)
            pop_small()
            s += 1
